import numpy as np
import ml_dtypes


def mxq(x, axis, fmt="e4m3"):
    dtype, down = {"e4m3": (ml_dtypes.float8_e4m3fn, 7), "e5m2": (ml_dtypes.float8_e5m2, 14)}[fmt]
    v = np.moveaxis(np.asarray(x, np.float32).astype(ml_dtypes.bfloat16).astype(np.float64), axis, -1)
    blocks = v.reshape(v.shape[:-1] + (-1, 32))
    amax = np.abs(blocks).max(-1, keepdims=True)
    byte = np.maximum(np.where(amax > 0, np.frexp(amax)[1] - 1 + 127, 0) - down, 1)
    scale = np.exp2(byte - 127.0)
    codes = (blocks / scale).astype(np.float32).astype(dtype).astype(np.float64)
    return np.moveaxis((codes * scale).reshape(v.shape), -1, axis)


WIDE = False


def mx_kscale(k):
    if not WIDE:
        return np.ones(k)
    levels = np.array([10, -10, 5, -5, 0])
    a = np.random.permutation(np.resize(levels, k // 512 * 4)).reshape(k // 512, 4)
    idx = np.arange(k)
    return np.exp2(a[idx // 512, idx % 128 // 32])


BF16 = ml_dtypes.bfloat16


def bf(x):
    return np.asarray(x, np.float32).astype(BF16)


def f64(x):
    return np.asarray(x).astype(np.float64)


B, DIM, DI, H, W = 4, 512, 512, 32, 16
N = H * W
EPS = 1e-5
A = 2.0


def setup_inputs():
    s, t = mx_kscale(DI), mx_kscale(DI)
    return {"attention": bf(np.random.standard_normal((B, DI, DI)) * A * A * np.sqrt(N) / DI * t[None, :, None] * s[None, None, :]),
            "g_x": bf(np.random.standard_normal((B, DI, N)) / s[None, :, None]),
            "x": bf(np.random.standard_normal((B, DIM, H, W))),
            "Ww": bf(np.random.standard_normal((DIM, DI)) * 0.5 / np.sqrt(DI) / t[None, :]),
            "bw": bf(np.random.standard_normal(DIM) * 0.5),
            "gamma": bf(np.random.standard_normal(DIM) * 0.3),
            "beta": bf(np.random.standard_normal(DIM) * 0.3),
            "run_mean": bf(np.random.standard_normal(DIM) * 0.5),
            "run_var": bf(np.random.uniform(0.5, 1.5, DIM))}


def reference(attention, g_x, x, Ww, bw, gamma, beta, run_mean, run_var):
    y = mxq(f64(attention), 2, "e4m3") @ mxq(f64(g_x), 1, "e4m3")
    W_y = (mxq(f64(Ww), 1, "e4m3") @ mxq(y, 1, "e4m3")) + f64(bw)[None, :, None]
    inv = f64(gamma) / np.sqrt(f64(run_var) + EPS)
    W_y = (W_y - f64(run_mean)[None, :, None]) * inv[None, :, None] + f64(beta)[None, :, None]
    return W_y.reshape(B, DIM, H, W) + f64(x)

@@ -1,0 +1,198 @@
+from contextlib import ExitStack
+
+import concourse.mybir as mybir
+from concourse.masks import make_identity
+
+BF16 = mybir.dt.bfloat16
+F32 = mybir.dt.float32
+U32 = mybir.dt.uint32
+U8 = mybir.dt.uint8
+FP8X4 = mybir.dt.float8_e4m3fn_x4
+ALU = mybir.AluOpType
+ACT = mybir.ActivationFunctionType
+
+P = 128
+PACK = 4
+K = P * PACK
+IMAGES = 4
+CHANNELS = 512
+POSITIONS = 512
+ROW_TILES = CHANNELS // P
+EPS = 1e-5
+
+FLOPS = 2 * IMAGES * (CHANNELS * K * POSITIONS + CHANNELS * K * POSITIONS)
+
+
+def k_pairs_view(rows_in_dram):
+    return rows_in_dram.rearrange("(u p e) w -> p u e w", u=2, e=2)
+
+
+def move_k_onto_partitions(nc, psum, identity, rows, grouped):
+    grouped_words = grouped.bitcast(F32).rearrange("p (c u) -> p c u", u=2)
+    tiles_in_bank = 2
+    for first in range(0, ROW_TILES, tiles_in_bank):
+        bank = psum.tile([P, 2, tiles_in_bank * P], F32, tag="transposed")
+        for r in range(first, first + tiles_in_bank):
+            words = rows[:, r, :].bitcast(F32)
+            for u in range(2):
+                nc.tensor.transpose(
+                    bank[:, u, (r - first) * P : (r - first + 1) * P],
+                    words[:, u * P : (u + 1) * P],
+                    identity,
+                )
+        nc.scalar.copy(
+            out=grouped_words[:, first * P : (first + tiles_in_bank) * P, :],
+            in_=bank[:].rearrange("p u c -> p c u"),
+        )
+
+
+def tile_cnl_pb_kernel(
+    tc, attention, g_x, x, Ww, bw, gamma, beta, run_mean, run_var, out
+):
+    nc = tc.nc
+    with ExitStack() as ctx:
+        const = ctx.enter_context(tc.tile_pool(name="const", bufs=1))
+        resident = ctx.enter_context(tc.tile_pool(name="resident", bufs=IMAGES))
+        work = ctx.enter_context(tc.tile_pool(name="work", bufs=2))
+        psum_t = ctx.enter_context(tc.psum_pool(name="psum_t", bufs=2))
+        psum_y = ctx.enter_context(tc.psum_pool(name="psum_y", bufs=3))
+        psum_z = ctx.enter_context(tc.psum_pool(name="psum_z", bufs=3))
+
+        att_tiles, g_tiles, x_tiles = [], [], []
+        w_rows = const.tile([P, ROW_TILES, K], BF16)
+        for b in range(IMAGES):
+            att_rows = resident.tile([P, PACK, K], BF16)
+            nc.sync.dma_start(
+                out=att_rows[:].rearrange("p (u e) k -> p u e k", u=2),
+                in_=k_pairs_view(attention[b]),
+            )
+            g_rows = resident.tile([P, PACK, POSITIONS], BF16)
+            nc.sync.dma_start(
+                out=g_rows[:].rearrange("p (u e) n -> p u e n", u=2),
+                in_=k_pairs_view(g_x[b]),
+            )
+            if b == 0:
+                nc.sync.dma_start(
+                    out=w_rows[:], in_=Ww.rearrange("(p ct) k -> p ct k", ct=ROW_TILES)
+                )
+            x_rows = resident.tile([P, ROW_TILES, POSITIONS], BF16)
+            nc.sync.dma_start(
+                out=x_rows[:], in_=x[b].rearrange("(p ct) h w -> p ct (h w)", ct=ROW_TILES)
+            )
+            att_tiles.append(att_rows)
+            g_tiles.append(g_rows)
+            x_tiles.append(x_rows)
+
+        per_channel = {}
+        for name, vector in (
+            ("run_var", run_var),
+            ("gamma", gamma),
+            ("bw", bw),
+            ("run_mean", run_mean),
+            ("beta", beta),
+        ):
+            per_channel[name] = const.tile([P, ROW_TILES], BF16, name=name)
+            nc.scalar.dma_start(
+                out=per_channel[name][:], in_=vector.rearrange("(p ct) -> p ct", ct=ROW_TILES)
+            )
+
+        identity = const.tile([P, P], F32)
+        make_identity(nc, identity[:])
+
+        gain = const.tile([P, ROW_TILES], F32)
+        shift = const.tile([P, ROW_TILES], F32)
+        nc.vector.tensor_scalar_add(gain[:], per_channel["run_var"][:], EPS)
+        nc.scalar.sqrt(gain[:], gain[:])
+        nc.vector.reciprocal(gain[:], gain[:])
+        nc.vector.tensor_mul(gain[:], gain[:], per_channel["gamma"][:])
+        nc.vector.tensor_sub(shift[:], per_channel["bw"][:], per_channel["run_mean"][:])
+        nc.vector.tensor_mul(shift[:], shift[:], gain[:])
+        nc.vector.tensor_add(shift[:], shift[:], per_channel["beta"][:])
+
+        w_grouped = const.tile([P, CHANNELS * PACK], BF16, align_bytes=64)
+        w_codes = const.tile([P, CHANNELS], U32, align_bytes=64)
+        w_scales = const.tile([P, CHANNELS], U8, align_bytes=64)
+
+        def quantise(codes, scales, grouped):
+            nc.vector.quantize_mx(out=codes.bitcast(FP8X4), scales=scales, in_=grouped)
+
+        def prepare(b):
+            att_grouped = work.tile([P, CHANNELS * PACK], BF16, align_bytes=64)
+            move_k_onto_partitions(nc, psum_t, identity[:], att_tiles[b], att_grouped[:])
+            g_grouped = work.tile([P, POSITIONS, PACK], BF16, align_bytes=64)
+            nc.vector.tensor_copy(
+                out=g_grouped[:].rearrange("p (c i) t -> p c t i", i=4),
+                in_=g_tiles[b][:].rearrange("p t (c i) -> p c t i", i=4),
+            )
+            att_codes = work.tile([P, CHANNELS], U32, align_bytes=64)
+            att_scales = work.tile([P, CHANNELS], U8, align_bytes=64)
+            quantise(att_codes[:], att_scales[:], att_grouped[:])
+            g_codes = work.tile([P, POSITIONS], U32, align_bytes=64)
+            g_scales = work.tile([P, POSITIONS], U8, align_bytes=64)
+            quantise(g_codes[:], g_scales[:], g_grouped[:].rearrange("p n t -> p (n t)"))
+            result = resident.tile([P, ROW_TILES, POSITIONS], F32)
+            for ct in range(ROW_TILES):
+                nc.scalar.activation(
+                    out=result[:, ct, :],
+                    in_=x_tiles[b][:, ct, :],
+                    func=ACT.Identity,
+                    bias=shift[:, ct : ct + 1],
+                    scale=1.0,
+                )
+            return att_codes, att_scales, g_codes, g_scales, result
+
+        def first_product(att_codes, att_scales, g_codes, g_scales):
+            y_grouped = work.tile([P, POSITIONS, PACK], BF16, align_bytes=64)
+            for n0 in range(0, POSITIONS, P):
+                y_bank = psum_y.tile([P, PACK, P], F32)
+                for t in range(PACK):
+                    nc.tensor.matmul_mx(
+                        out=y_bank[:, t, :],
+                        lhsT=att_codes[:, t * P : (t + 1) * P].bitcast(FP8X4),
+                        lhsT_scale=att_scales[:, t * P : (t + 1) * P],
+                        rhs=g_codes[:, n0 : n0 + P].bitcast(FP8X4),
+                        rhs_scale=g_scales[:, n0 : n0 + P],
+                        start=True,
+                        stop=True,
+                    )
+                nc.scalar.copy(
+                    out=y_grouped[:, n0 : n0 + P, :], in_=y_bank[:].rearrange("p t n -> p n t")
+                )
+            y_codes = work.tile([P, POSITIONS], U32, align_bytes=64)
+            y_scales = work.tile([P, POSITIONS], U8, align_bytes=64)
+            quantise(y_codes[:], y_scales[:], y_grouped[:].rearrange("p n t -> p (n t)"))
+            return y_codes, y_scales
+
+        def second_product(b, y_codes, y_scales, result):
+            for ct in range(ROW_TILES):
+                z_bank = psum_z.tile([P, POSITIONS], F32)
+                nc.tensor.matmul_mx(
+                    out=z_bank[:],
+                    lhsT=w_codes[:, ct * P : (ct + 1) * P].bitcast(FP8X4),
+                    lhsT_scale=w_scales[:, ct * P : (ct + 1) * P],
+                    rhs=y_codes[:].bitcast(FP8X4),
+                    rhs_scale=y_scales[:],
+                    start=True,
+                    stop=True,
+                )
+                nc.vector.scalar_tensor_tensor(
+                    out=result[:, ct, :],
+                    in0=z_bank[:],
+                    scalar=gain[:, ct : ct + 1],
+                    in1=result[:, ct, :],
+                    op0=ALU.mult,
+                    op1=ALU.add,
+                )
+            nc.sync.dma_start(
+                out=out[b].rearrange("(p ct) h w -> p ct (h w)", ct=ROW_TILES), in_=result[:]
+            )
+
+        prepared = prepare(0)
+        move_k_onto_partitions(nc, psum_t, identity[:], w_rows, w_grouped[:])
+        quantise(w_codes[:], w_scales[:], w_grouped[:])
+        for b in range(IMAGES):
+            att_codes, att_scales, g_codes, g_scales, result = prepared
+            if b + 1 < IMAGES:
+                prepared = prepare(b + 1)
+            y_codes, y_scales = first_product(att_codes, att_scales, g_codes, g_scales)
+            second_product(b, y_codes, y_scales, result)

@@ -19,31 +19,13 @@ CHANNELS = 512
 POSITIONS = 512
 ROW_TILES = CHANNELS // P
 EPS = 1e-5
+TILES_ON_VECTOR = 1
 
 FLOPS = 2 * IMAGES * (CHANNELS * K * POSITIONS + CHANNELS * K * POSITIONS)
 
 
 def k_pairs_view(rows_in_dram):
     return rows_in_dram.rearrange("(u p e) w -> p u e w", u=2, e=2)
-
-
-def move_k_onto_partitions(nc, psum, identity, rows, grouped):
-    grouped_words = grouped.bitcast(F32).rearrange("p (c u) -> p c u", u=2)
-    tiles_in_bank = 2
-    for first in range(0, ROW_TILES, tiles_in_bank):
-        bank = psum.tile([P, 2, tiles_in_bank * P], F32, tag="transposed")
-        for r in range(first, first + tiles_in_bank):
-            words = rows[:, r, :].bitcast(F32)
-            for u in range(2):
-                nc.tensor.transpose(
-                    bank[:, u, (r - first) * P : (r - first + 1) * P],
-                    words[:, u * P : (u + 1) * P],
-                    identity,
-                )
-        nc.scalar.copy(
-            out=grouped_words[:, first * P : (first + tiles_in_bank) * P, :],
-            in_=bank[:].rearrange("p u c -> p c u"),
-        )
 
 
 def tile_cnl_pb_kernel(
@@ -55,33 +37,9 @@ def tile_cnl_pb_kernel(
         resident = ctx.enter_context(tc.tile_pool(name="resident", bufs=IMAGES))
         work = ctx.enter_context(tc.tile_pool(name="work", bufs=2))
         psum_t = ctx.enter_context(tc.psum_pool(name="psum_t", bufs=2))
-        psum_y = ctx.enter_context(tc.psum_pool(name="psum_y", bufs=3))
-        psum_z = ctx.enter_context(tc.psum_pool(name="psum_z", bufs=3))
-
-        att_tiles, g_tiles, x_tiles = [], [], []
-        w_rows = const.tile([P, ROW_TILES, K], BF16)
-        for b in range(IMAGES):
-            att_rows = resident.tile([P, PACK, K], BF16)
-            nc.sync.dma_start(
-                out=att_rows[:].rearrange("p (u e) k -> p u e k", u=2),
-                in_=k_pairs_view(attention[b]),
-            )
-            g_rows = resident.tile([P, PACK, POSITIONS], BF16)
-            nc.sync.dma_start(
-                out=g_rows[:].rearrange("p (u e) n -> p u e n", u=2),
-                in_=k_pairs_view(g_x[b]),
-            )
-            if b == 0:
-                nc.sync.dma_start(
-                    out=w_rows[:], in_=Ww.rearrange("(p ct) k -> p ct k", ct=ROW_TILES)
-                )
-            x_rows = resident.tile([P, ROW_TILES, POSITIONS], BF16)
-            nc.sync.dma_start(
-                out=x_rows[:], in_=x[b].rearrange("(p ct) h w -> p ct (h w)", ct=ROW_TILES)
-            )
-            att_tiles.append(att_rows)
-            g_tiles.append(g_rows)
-            x_tiles.append(x_rows)
+        psum_y = ctx.enter_context(tc.psum_pool(name="psum_y", bufs=2))
+        psum_z = ctx.enter_context(tc.psum_pool(name="psum_z", bufs=ROW_TILES))
+        ctx.enter_context(tc.manual_schedule())
 
         per_channel = {}
         for name, vector in (
@@ -96,103 +54,194 @@ def tile_cnl_pb_kernel(
                 out=per_channel[name][:], in_=vector.rearrange("(p ct) -> p ct", ct=ROW_TILES)
             )
 
+        warm = const.tile([P, 1], F32)
+        nc.vector.memset(warm[:], 1.0)
+        nc.scalar.sqrt(warm[:], warm[:])
+
+        att_tiles, g_tiles, x_tiles = [], [], []
+        for b in range(IMAGES):
+            att_low = resident.tile([P, 2, K], BF16)
+            att_high = resident.tile([P, 2, K], BF16)
+            g_rows = resident.tile([P, PACK, POSITIONS], BF16)
+            x_rows = resident.tile([P, ROW_TILES, POSITIONS], BF16)
+            att_tiles.append((att_low, att_high))
+            g_tiles.append(g_rows)
+            x_tiles.append(x_rows)
+        w_rows = const.tile([P, ROW_TILES, K], BF16)
+
+        def load_attention(b, u):
+            nc.sync.dma_start(out=att_tiles[b][u][:], in_=k_pairs_view(attention[b])[:, u, :, :])
+
+        def load_g(b):
+            nc.sync.dma_start(
+                out=g_tiles[b][:].rearrange("p (u e) n -> p u e n", u=2),
+                in_=k_pairs_view(g_x[b]),
+            )
+
+        def load_x(b):
+            nc.sync.dma_start(
+                out=x_tiles[b][:],
+                in_=x[b].rearrange("(p ct) h w -> p ct (h w)", ct=ROW_TILES),
+            )
+
+        load_attention(0, 0)
+        load_g(0)
+        load_attention(0, 1)
+        nc.sync.dma_start(out=w_rows[:], in_=Ww.rearrange("(p ct) k -> p ct k", ct=ROW_TILES))
+        load_x(0)
+        for b in range(1, IMAGES):
+            load_g(b)
+            load_attention(b, 0)
+            load_attention(b, 1)
+            load_x(b)
+
         identity = const.tile([P, P], F32)
         make_identity(nc, identity[:])
 
         gain = const.tile([P, ROW_TILES], F32)
         shift = const.tile([P, ROW_TILES], F32)
-        nc.vector.tensor_scalar_add(gain[:], per_channel["run_var"][:], EPS)
-        nc.scalar.sqrt(gain[:], gain[:])
-        nc.vector.reciprocal(gain[:], gain[:])
-        nc.vector.tensor_mul(gain[:], gain[:], per_channel["gamma"][:])
-        nc.vector.tensor_sub(shift[:], per_channel["bw"][:], per_channel["run_mean"][:])
-        nc.vector.tensor_mul(shift[:], shift[:], gain[:])
-        nc.vector.tensor_add(shift[:], shift[:], per_channel["beta"][:])
-
         w_grouped = const.tile([P, CHANNELS * PACK], BF16, align_bytes=64)
         w_codes = const.tile([P, CHANNELS], U32, align_bytes=64)
         w_scales = const.tile([P, CHANNELS], U8, align_bytes=64)
 
-        def quantise(codes, scales, grouped):
-            nc.vector.quantize_mx(out=codes.bitcast(FP8X4), scales=scales, in_=grouped)
+        def transpose_words(halves):
+            banks = []
+            for rows in halves:
+                bank = psum_t.tile([P, 2, 2 * P], F32)
+                for r in range(2):
+                    words = rows[:, r, :].bitcast(F32)
+                    for u in range(2):
+                        nc.tensor.transpose(
+                            bank[:, u, r * P : (r + 1) * P], words[:, u * P : (u + 1) * P], identity[:]
+                        )
+                banks.append(bank)
+            return banks
 
-        def prepare(b):
-            att_grouped = work.tile([P, CHANNELS * PACK], BF16, align_bytes=64)
-            move_k_onto_partitions(nc, psum_t, identity[:], att_tiles[b], att_grouped[:])
+        def interleave_halves(banks, grouped):
+            grouped_words = grouped.bitcast(F32).rearrange("p (c u) -> p c u", u=2)
+            for h, bank in enumerate(banks):
+                nc.scalar.copy(
+                    out=grouped_words[:, h * 2 * P : (h + 1) * 2 * P, :],
+                    in_=bank[:].rearrange("p u c -> p c u"),
+                )
+
+        def quantise(grouped, operand):
+            codes = work.tile([P, CHANNELS], U32, align_bytes=64, name=operand + "_codes")
+            scales = work.tile([P, CHANNELS], U8, align_bytes=64, name=operand + "_scales")
+            nc.vector.quantize_mx(out=codes[:].bitcast(FP8X4), scales=scales[:], in_=grouped)
+            return codes, scales
+
+        def regroup_g(b):
             g_grouped = work.tile([P, POSITIONS, PACK], BF16, align_bytes=64)
             nc.vector.tensor_copy(
                 out=g_grouped[:].rearrange("p (c i) t -> p c t i", i=4),
                 in_=g_tiles[b][:].rearrange("p t (c i) -> p c t i", i=4),
             )
-            att_codes = work.tile([P, CHANNELS], U32, align_bytes=64)
-            att_scales = work.tile([P, CHANNELS], U8, align_bytes=64)
-            quantise(att_codes[:], att_scales[:], att_grouped[:])
-            g_codes = work.tile([P, POSITIONS], U32, align_bytes=64)
-            g_scales = work.tile([P, POSITIONS], U8, align_bytes=64)
-            quantise(g_codes[:], g_scales[:], g_grouped[:].rearrange("p n t -> p (n t)"))
-            result = resident.tile([P, ROW_TILES, POSITIONS], F32)
-            for ct in range(ROW_TILES):
-                nc.scalar.activation(
-                    out=result[:, ct, :],
-                    in_=x_tiles[b][:, ct, :],
-                    func=ACT.Identity,
-                    bias=shift[:, ct : ct + 1],
-                    scale=1.0,
-                )
-            return att_codes, att_scales, g_codes, g_scales, result
+            return g_grouped
 
-        def first_product(att_codes, att_scales, g_codes, g_scales):
+        def add_shift(b, result, channel_tiles):
+            for ct in channel_tiles:
+                if ct < TILES_ON_VECTOR:
+                    nc.vector.tensor_scalar_add(
+                        result[:, ct, :], x_tiles[b][:, ct, :], shift[:, ct : ct + 1]
+                    )
+                else:
+                    nc.scalar.activation(
+                        out=result[:, ct, :],
+                        in_=x_tiles[b][:, ct, :],
+                        func=ACT.Identity,
+                        bias=shift[:, ct : ct + 1],
+                        scale=1.0,
+                    )
+
+        def first_product(att_q, g_q):
             y_grouped = work.tile([P, POSITIONS, PACK], BF16, align_bytes=64)
             for n0 in range(0, POSITIONS, P):
                 y_bank = psum_y.tile([P, PACK, P], F32)
                 for t in range(PACK):
                     nc.tensor.matmul_mx(
                         out=y_bank[:, t, :],
-                        lhsT=att_codes[:, t * P : (t + 1) * P].bitcast(FP8X4),
-                        lhsT_scale=att_scales[:, t * P : (t + 1) * P],
-                        rhs=g_codes[:, n0 : n0 + P].bitcast(FP8X4),
-                        rhs_scale=g_scales[:, n0 : n0 + P],
+                        lhsT=att_q[0][:, t * P : (t + 1) * P].bitcast(FP8X4),
+                        lhsT_scale=att_q[1][:, t * P : (t + 1) * P],
+                        rhs=g_q[0][:, n0 : n0 + P].bitcast(FP8X4),
+                        rhs_scale=g_q[1][:, n0 : n0 + P],
                         start=True,
                         stop=True,
                     )
                 nc.scalar.copy(
                     out=y_grouped[:, n0 : n0 + P, :], in_=y_bank[:].rearrange("p t n -> p n t")
                 )
-            y_codes = work.tile([P, POSITIONS], U32, align_bytes=64)
-            y_scales = work.tile([P, POSITIONS], U8, align_bytes=64)
-            quantise(y_codes[:], y_scales[:], y_grouped[:].rearrange("p n t -> p (n t)"))
-            return y_codes, y_scales
+            return y_grouped
 
-        def second_product(b, y_codes, y_scales, result):
+        def second_product(y_q):
+            z_banks = []
             for ct in range(ROW_TILES):
                 z_bank = psum_z.tile([P, POSITIONS], F32)
                 nc.tensor.matmul_mx(
                     out=z_bank[:],
                     lhsT=w_codes[:, ct * P : (ct + 1) * P].bitcast(FP8X4),
                     lhsT_scale=w_scales[:, ct * P : (ct + 1) * P],
-                    rhs=y_codes[:].bitcast(FP8X4),
-                    rhs_scale=y_scales[:],
+                    rhs=y_q[0][:].bitcast(FP8X4),
+                    rhs_scale=y_q[1][:],
                     start=True,
                     stop=True,
                 )
+                z_banks.append(z_bank)
+            return z_banks
+
+        def finish(b, z_banks, result):
+            out_b = out[b].rearrange("(p ct) h w -> p ct (h w)", ct=ROW_TILES)
+            for ct in range(ROW_TILES):
                 nc.vector.scalar_tensor_tensor(
                     out=result[:, ct, :],
-                    in0=z_bank[:],
+                    in0=z_banks[ct][:],
                     scalar=gain[:, ct : ct + 1],
                     in1=result[:, ct, :],
                     op0=ALU.mult,
                     op1=ALU.add,
                 )
-            nc.sync.dma_start(
-                out=out[b].rearrange("(p ct) h w -> p ct (h w)", ct=ROW_TILES), in_=result[:]
-            )
+                nc.sync.dma_start(out=out_b[:, ct, :], in_=result[:, ct, :])
 
-        prepared = prepare(0)
-        move_k_onto_partitions(nc, psum_t, identity[:], w_rows, w_grouped[:])
-        quantise(w_codes[:], w_scales[:], w_grouped[:])
+        vector_tiles = range(TILES_ON_VECTOR)
+        scalar_tiles = range(TILES_ON_VECTOR, ROW_TILES)
+
+        nc.vector.tensor_scalar_add(gain[:], per_channel["run_var"][:], EPS)
+        nc.scalar.sqrt(gain[:], gain[:])
+        nc.vector.tensor_sub(shift[:], per_channel["bw"][:], per_channel["run_mean"][:])
+        nc.vector.reciprocal(gain[:], gain[:])
+        nc.vector.tensor_mul(gain[:], gain[:], per_channel["gamma"][:])
+        nc.vector.tensor_mul(shift[:], shift[:], gain[:])
+        nc.vector.tensor_add(shift[:], shift[:], per_channel["beta"][:])
+        att_banks = transpose_words(att_tiles[0])
+        att_grouped = work.tile([P, CHANNELS * PACK], BF16, align_bytes=64)
+        interleave_halves(att_banks, att_grouped[:])
+        g_grouped = regroup_g(0)
+        g_q = quantise(g_grouped[:].rearrange("p n t -> p (n t)"), "g")
+        att_q = quantise(att_grouped[:], "att")
+        w_banks = transpose_words((w_rows[:, 0:2, :], w_rows[:, 2:4, :]))
+        interleave_halves(w_banks, w_grouped[:])
+        nc.vector.quantize_mx(out=w_codes[:].bitcast(FP8X4), scales=w_scales[:], in_=w_grouped[:])
+        result = resident.tile([P, ROW_TILES, POSITIONS], F32)
+        add_shift(0, result, vector_tiles)
+        g_grouped = regroup_g(1)
+        y_grouped = first_product(att_q, g_q)
+        att_banks = transpose_words(att_tiles[1])
+
         for b in range(IMAGES):
-            att_codes, att_scales, g_codes, g_scales, result = prepared
+            y_q = quantise(y_grouped[:].rearrange("p n t -> p (n t)"), "y")
             if b + 1 < IMAGES:
-                prepared = prepare(b + 1)
-            y_codes, y_scales = first_product(att_codes, att_scales, g_codes, g_scales)
-            second_product(b, y_codes, y_scales, result)
+                g_q = quantise(g_grouped[:].rearrange("p n t -> p (n t)"), "g")
+                att_grouped = work.tile([P, CHANNELS * PACK], BF16, align_bytes=64)
+                interleave_halves(att_banks, att_grouped[:])
+                att_q = quantise(att_grouped[:], "att")
+            add_shift(b, result, scalar_tiles)
+            z_banks = second_product(y_q)
+            finish(b, z_banks, result)
+            if b + 2 < IMAGES:
+                g_grouped = regroup_g(b + 2)
+            if b + 1 < IMAGES:
+                result = resident.tile([P, ROW_TILES, POSITIONS], F32)
+                add_shift(b + 1, result, vector_tiles)
+                y_grouped = first_product(att_q, g_q)
+            if b + 2 < IMAGES:
+                att_banks = transpose_words(att_tiles[b + 2])

@@ -36,8 +36,7 @@ def tile_cnl_pb_kernel(
         const = ctx.enter_context(tc.tile_pool(name="const", bufs=1))
         resident = ctx.enter_context(tc.tile_pool(name="resident", bufs=IMAGES))
         work = ctx.enter_context(tc.tile_pool(name="work", bufs=2))
-        psum_t = ctx.enter_context(tc.psum_pool(name="psum_t", bufs=2))
-        psum_y = ctx.enter_context(tc.psum_pool(name="psum_y", bufs=2))
+        psum_front = ctx.enter_context(tc.psum_pool(name="psum_front", bufs=4))
         psum_z = ctx.enter_context(tc.psum_pool(name="psum_z", bufs=ROW_TILES))
         ctx.enter_context(tc.manual_schedule())
 
@@ -88,12 +87,16 @@ def tile_cnl_pb_kernel(
         load_g(0)
         load_attention(0, 1)
         nc.sync.dma_start(out=w_rows[:], in_=Ww.rearrange("(p ct) k -> p ct k", ct=ROW_TILES))
+        load_attention(1, 0)
+        load_attention(1, 1)
+        load_g(1)
         load_x(0)
-        for b in range(1, IMAGES):
+        for b in range(2, IMAGES):
             load_g(b)
             load_attention(b, 0)
             load_attention(b, 1)
-            load_x(b)
+            load_x(b - 1)
+        load_x(IMAGES - 1)
 
         identity = const.tile([P, P], F32)
         make_identity(nc, identity[:])
@@ -107,7 +110,7 @@ def tile_cnl_pb_kernel(
         def transpose_words(halves):
             banks = []
             for rows in halves:
-                bank = psum_t.tile([P, 2, 2 * P], F32)
+                bank = psum_front.tile([P, 2, 2 * P], F32, tag="front")
                 for r in range(2):
                     words = rows[:, r, :].bitcast(F32)
                     for u in range(2):
@@ -155,9 +158,9 @@ def tile_cnl_pb_kernel(
                     )
 
         def first_product(att_q, g_q):
-            y_grouped = work.tile([P, POSITIONS, PACK], BF16, align_bytes=64)
+            y_banks = []
             for n0 in range(0, POSITIONS, P):
-                y_bank = psum_y.tile([P, PACK, P], F32)
+                y_bank = psum_front.tile([P, PACK, P], F32, tag="front")
                 for t in range(PACK):
                     nc.tensor.matmul_mx(
                         out=y_bank[:, t, :],
@@ -168,8 +171,15 @@ def tile_cnl_pb_kernel(
                         start=True,
                         stop=True,
                     )
+                y_banks.append(y_bank)
+            return y_banks
+
+        def round_y(y_banks):
+            y_grouped = work.tile([P, POSITIONS, PACK], BF16, align_bytes=64)
+            for q, y_bank in enumerate(y_banks):
                 nc.scalar.copy(
-                    out=y_grouped[:, n0 : n0 + P, :], in_=y_bank[:].rearrange("p t n -> p n t")
+                    out=y_grouped[:, q * P : (q + 1) * P, :],
+                    in_=y_bank[:].rearrange("p t n -> p n t"),
                 )
             return y_grouped
 
@@ -205,6 +215,22 @@ def tile_cnl_pb_kernel(
         vector_tiles = range(TILES_ON_VECTOR)
         scalar_tiles = range(TILES_ON_VECTOR, ROW_TILES)
 
+        def group_attention(att_banks):
+            att_grouped = work.tile([P, CHANNELS * PACK], BF16, align_bytes=64)
+            interleave_halves(att_banks, att_grouped[:])
+            return att_grouped
+
+        def quantise_g(g_grouped):
+            return quantise(g_grouped[:].rearrange("p n t -> p (n t)"), "g")
+
+        operands = {}
+        results = {}
+        for b in range(IMAGES):
+            results[b] = resident.tile([P, ROW_TILES, POSITIONS], F32, name="result")
+        att_grouped = group_attention(transpose_words(att_tiles[0]))
+        g_grouped = regroup_g(0)
+        g_q = quantise_g(g_grouped)
+        operands[0] = (quantise(att_grouped[:], "att"), g_q)
         nc.vector.tensor_scalar_add(gain[:], per_channel["run_var"][:], EPS)
         nc.scalar.sqrt(gain[:], gain[:])
         nc.vector.tensor_sub(shift[:], per_channel["bw"][:], per_channel["run_mean"][:])
@@ -212,36 +238,31 @@ def tile_cnl_pb_kernel(
         nc.vector.tensor_mul(gain[:], gain[:], per_channel["gamma"][:])
         nc.vector.tensor_mul(shift[:], shift[:], gain[:])
         nc.vector.tensor_add(shift[:], shift[:], per_channel["beta"][:])
-        att_banks = transpose_words(att_tiles[0])
-        att_grouped = work.tile([P, CHANNELS * PACK], BF16, align_bytes=64)
-        interleave_halves(att_banks, att_grouped[:])
-        g_grouped = regroup_g(0)
-        g_q = quantise(g_grouped[:].rearrange("p n t -> p (n t)"), "g")
-        att_q = quantise(att_grouped[:], "att")
         w_banks = transpose_words((w_rows[:, 0:2, :], w_rows[:, 2:4, :]))
         interleave_halves(w_banks, w_grouped[:])
         nc.vector.quantize_mx(out=w_codes[:].bitcast(FP8X4), scales=w_scales[:], in_=w_grouped[:])
-        result = resident.tile([P, ROW_TILES, POSITIONS], F32)
-        add_shift(0, result, vector_tiles)
+        att_grouped = group_attention(transpose_words(att_tiles[1]))
         g_grouped = regroup_g(1)
-        y_grouped = first_product(att_q, g_q)
-        att_banks = transpose_words(att_tiles[1])
+        g_q = quantise_g(g_grouped)
+        operands[1] = (quantise(att_grouped[:], "att"), g_q)
+        g_grouped = regroup_g(2)
+        add_shift(0, results[0], vector_tiles)
+        y_banks = first_product(operands[0][0], operands[0][1])
 
         for b in range(IMAGES):
+            y_grouped = round_y(y_banks)
+            if b + 2 < IMAGES:
+                att_grouped = group_attention(transpose_words(att_tiles[b + 2]))
+            if b + 1 < IMAGES:
+                y_banks = first_product(operands[b + 1][0], operands[b + 1][1])
             y_q = quantise(y_grouped[:].rearrange("p n t -> p (n t)"), "y")
+            if b + 2 < IMAGES:
+                g_q = quantise_g(g_grouped)
+                operands[b + 2] = (quantise(att_grouped[:], "att"), g_q)
+            add_shift(b, results[b], scalar_tiles)
             if b + 1 < IMAGES:
-                g_q = quantise(g_grouped[:].rearrange("p n t -> p (n t)"), "g")
-                att_grouped = work.tile([P, CHANNELS * PACK], BF16, align_bytes=64)
-                interleave_halves(att_banks, att_grouped[:])
-                att_q = quantise(att_grouped[:], "att")
-            add_shift(b, result, scalar_tiles)
+                add_shift(b + 1, results[b + 1], vector_tiles)
             z_banks = second_product(y_q)
-            finish(b, z_banks, result)
-            if b + 2 < IMAGES:
-                g_grouped = regroup_g(b + 2)
-            if b + 1 < IMAGES:
-                result = resident.tile([P, ROW_TILES, POSITIONS], F32)
-                add_shift(b + 1, result, vector_tiles)
-                y_grouped = first_product(att_q, g_q)
-            if b + 2 < IMAGES:
-                att_banks = transpose_words(att_tiles[b + 2])
+            finish(b, z_banks, results[b])
+            if b + 3 < IMAGES:
+                g_grouped = regroup_g(b + 3)

@@ -20,6 +20,7 @@ POSITIONS = 512
 ROW_TILES = CHANNELS // P
 EPS = 1e-5
 TILES_ON_VECTOR = 1
+EARLY_TILES = 2
 
 FLOPS = 2 * IMAGES * (CHANNELS * K * POSITIONS + CHANNELS * K * POSITIONS)
 
@@ -59,17 +60,19 @@ def tile_cnl_pb_kernel(
 
         att_tiles, g_tiles, x_tiles = [], [], []
         for b in range(IMAGES):
-            att_low = resident.tile([P, 2, K], BF16)
-            att_high = resident.tile([P, 2, K], BF16)
+            att_rows = resident.tile([P, PACK, K], BF16)
             g_rows = resident.tile([P, PACK, POSITIONS], BF16)
             x_rows = resident.tile([P, ROW_TILES, POSITIONS], BF16)
-            att_tiles.append((att_low, att_high))
+            att_tiles.append(att_rows)
             g_tiles.append(g_rows)
             x_tiles.append(x_rows)
         w_rows = const.tile([P, ROW_TILES, K], BF16)
 
-        def load_attention(b, u):
-            nc.sync.dma_start(out=att_tiles[b][u][:], in_=k_pairs_view(attention[b])[:, u, :, :])
+        def load_attention(b):
+            nc.sync.dma_start(
+                out=att_tiles[b][:].rearrange("p (u e) k -> p u e k", u=2),
+                in_=k_pairs_view(attention[b]),
+            )
 
         def load_g(b):
             nc.sync.dma_start(
@@ -83,19 +86,16 @@ def tile_cnl_pb_kernel(
                 in_=x[b].rearrange("(p ct) h w -> p ct (h w)", ct=ROW_TILES),
             )
 
-        load_attention(0, 0)
+        load_attention(0)
         load_g(0)
-        load_attention(0, 1)
         nc.sync.dma_start(out=w_rows[:], in_=Ww.rearrange("(p ct) k -> p ct k", ct=ROW_TILES))
-        load_attention(1, 0)
-        load_attention(1, 1)
+        load_attention(1)
         load_g(1)
-        load_x(0)
         for b in range(2, IMAGES):
             load_g(b)
-            load_attention(b, 0)
-            load_attention(b, 1)
-            load_x(b - 1)
+            load_attention(b)
+            load_x(b - 2)
+        load_x(IMAGES - 2)
         load_x(IMAGES - 1)
 
         identity = const.tile([P, P], F32)
@@ -107,12 +107,12 @@ def tile_cnl_pb_kernel(
         w_codes = const.tile([P, CHANNELS], U32, align_bytes=64)
         w_scales = const.tile([P, CHANNELS], U8, align_bytes=64)
 
-        def transpose_words(halves):
+        def transpose_words(rows):
             banks = []
-            for rows in halves:
+            for first in range(0, ROW_TILES, 2):
                 bank = psum_front.tile([P, 2, 2 * P], F32, tag="front")
                 for r in range(2):
-                    words = rows[:, r, :].bitcast(F32)
+                    words = rows[:, first + r, :].bitcast(F32)
                     for u in range(2):
                         nc.tensor.transpose(
                             bank[:, u, r * P : (r + 1) * P], words[:, u * P : (u + 1) * P], identity[:]
@@ -142,15 +142,15 @@ def tile_cnl_pb_kernel(
             )
             return g_grouped
 
-        def add_shift(b, result, channel_tiles):
+        def add_shift(b, channel_tiles, on_vector):
             for ct in channel_tiles:
-                if ct < TILES_ON_VECTOR:
+                if on_vector and ct < TILES_ON_VECTOR:
                     nc.vector.tensor_scalar_add(
-                        result[:, ct, :], x_tiles[b][:, ct, :], shift[:, ct : ct + 1]
+                        results[b][:, ct, :], x_tiles[b][:, ct, :], shift[:, ct : ct + 1]
                     )
-                else:
+                if not on_vector and ct >= TILES_ON_VECTOR:
                     nc.scalar.activation(
-                        out=result[:, ct, :],
+                        out=results[b][:, ct, :],
                         in_=x_tiles[b][:, ct, :],
                         func=ACT.Identity,
                         bias=shift[:, ct : ct + 1],
@@ -183,9 +183,8 @@ def tile_cnl_pb_kernel(
                 )
             return y_grouped
 
-        def second_product(y_q):
-            z_banks = []
-            for ct in range(ROW_TILES):
+        def second_product(b, y_q, channel_tiles):
+            for ct in channel_tiles:
                 z_bank = psum_z.tile([P, POSITIONS], F32)
                 nc.tensor.matmul_mx(
                     out=z_bank[:],
@@ -196,24 +195,23 @@ def tile_cnl_pb_kernel(
                     start=True,
                     stop=True,
                 )
-                z_banks.append(z_bank)
-            return z_banks
+                z_banks[(b, ct)] = z_bank
 
-        def finish(b, z_banks, result):
+        def finish(b, channel_tiles):
             out_b = out[b].rearrange("(p ct) h w -> p ct (h w)", ct=ROW_TILES)
-            for ct in range(ROW_TILES):
+            for ct in channel_tiles:
                 nc.vector.scalar_tensor_tensor(
-                    out=result[:, ct, :],
-                    in0=z_banks[ct][:],
+                    out=results[b][:, ct, :],
+                    in0=z_banks[(b, ct)][:],
                     scalar=gain[:, ct : ct + 1],
-                    in1=result[:, ct, :],
+                    in1=results[b][:, ct, :],
                     op0=ALU.mult,
                     op1=ALU.add,
                 )
-                nc.sync.dma_start(out=out_b[:, ct, :], in_=result[:, ct, :])
+                nc.sync.dma_start(out=out_b[:, ct, :], in_=results[b][:, ct, :])
 
-        vector_tiles = range(TILES_ON_VECTOR)
-        scalar_tiles = range(TILES_ON_VECTOR, ROW_TILES)
+        early = range(EARLY_TILES)
+        late = range(EARLY_TILES, ROW_TILES)
 
         def group_attention(att_banks):
             att_grouped = work.tile([P, CHANNELS * PACK], BF16, align_bytes=64)
@@ -224,6 +222,7 @@ def tile_cnl_pb_kernel(
             return quantise(g_grouped[:].rearrange("p n t -> p (n t)"), "g")
 
         operands = {}
+        z_banks = {}
         results = {}
         for b in range(IMAGES):
             results[b] = resident.tile([P, ROW_TILES, POSITIONS], F32, name="result")
@@ -238,31 +237,40 @@ def tile_cnl_pb_kernel(
         nc.vector.tensor_mul(gain[:], gain[:], per_channel["gamma"][:])
         nc.vector.tensor_mul(shift[:], shift[:], gain[:])
         nc.vector.tensor_add(shift[:], shift[:], per_channel["beta"][:])
-        w_banks = transpose_words((w_rows[:, 0:2, :], w_rows[:, 2:4, :]))
+        w_banks = transpose_words(w_rows)
         interleave_halves(w_banks, w_grouped[:])
+        g_grouped = regroup_g(1)
         nc.vector.quantize_mx(out=w_codes[:].bitcast(FP8X4), scales=w_scales[:], in_=w_grouped[:])
         att_grouped = group_attention(transpose_words(att_tiles[1]))
-        g_grouped = regroup_g(1)
         g_q = quantise_g(g_grouped)
         operands[1] = (quantise(att_grouped[:], "att"), g_q)
         g_grouped = regroup_g(2)
-        add_shift(0, results[0], vector_tiles)
         y_banks = first_product(operands[0][0], operands[0][1])
 
-        for b in range(IMAGES):
-            y_grouped = round_y(y_banks)
+        for b in range(IMAGES + 1):
+            if b < IMAGES:
+                y_grouped = round_y(y_banks)
             if b + 2 < IMAGES:
                 att_grouped = group_attention(transpose_words(att_tiles[b + 2]))
             if b + 1 < IMAGES:
                 y_banks = first_product(operands[b + 1][0], operands[b + 1][1])
-            y_q = quantise(y_grouped[:].rearrange("p n t -> p (n t)"), "y")
+            if b > 0:
+                add_shift(b - 1, late, False)
+            if b < IMAGES:
+                add_shift(b, early, False)
+                y_q = quantise(y_grouped[:].rearrange("p n t -> p (n t)"), "y")
             if b + 2 < IMAGES:
                 g_q = quantise_g(g_grouped)
                 operands[b + 2] = (quantise(att_grouped[:], "att"), g_q)
-            add_shift(b, results[b], scalar_tiles)
-            if b + 1 < IMAGES:
-                add_shift(b + 1, results[b + 1], vector_tiles)
-            z_banks = second_product(y_q)
-            finish(b, z_banks, results[b])
+            if b < IMAGES:
+                second_product(b, y_q, early)
+            if b > 0:
+                add_shift(b - 1, late, True)
+                finish(b - 1, late)
+            if b < IMAGES:
+                second_product(b, y_q, late)
             if b + 3 < IMAGES:
                 g_grouped = regroup_g(b + 3)
+            if b < IMAGES:
+                add_shift(b, early, True)
+                finish(b, early)

@@ -19,14 +19,14 @@ CHANNELS = 512
 POSITIONS = 512
 ROW_TILES = CHANNELS // P
 EPS = 1e-5
-TILES_ON_VECTOR = 1
+TILES_ON_VECTOR = 2
 EARLY_TILES = 2
 
 FLOPS = 2 * IMAGES * (CHANNELS * K * POSITIONS + CHANNELS * K * POSITIONS)
 
 
-def k_pairs_view(rows_in_dram):
-    return rows_in_dram.rearrange("(u p e) w -> p u e w", u=2, e=2)
+def k_on_partitions(rows_in_dram):
+    return rows_in_dram.rearrange("(p t) w -> p t w", t=PACK)
 
 
 def tile_cnl_pb_kernel(
@@ -69,16 +69,10 @@ def tile_cnl_pb_kernel(
         w_rows = const.tile([P, ROW_TILES, K], BF16)
 
         def load_attention(b):
-            nc.sync.dma_start(
-                out=att_tiles[b][:].rearrange("p (u e) k -> p u e k", u=2),
-                in_=k_pairs_view(attention[b]),
-            )
+            nc.sync.dma_start(out=att_tiles[b][:], in_=k_on_partitions(attention[b]))
 
         def load_g(b):
-            nc.sync.dma_start(
-                out=g_tiles[b][:].rearrange("p (u e) n -> p u e n", u=2),
-                in_=k_pairs_view(g_x[b]),
-            )
+            nc.sync.dma_start(out=g_tiles[b][:], in_=k_on_partitions(g_x[b]))
 
         def load_x(b):
             nc.sync.dma_start(
@@ -112,11 +106,9 @@ def tile_cnl_pb_kernel(
             for first in range(0, ROW_TILES, 2):
                 bank = psum_front.tile([P, 2, 2 * P], F32, tag="front")
                 for r in range(2):
-                    words = rows[:, first + r, :].bitcast(F32)
+                    words = rows[:, first + r, :].bitcast(F32).rearrange("m (p u) -> m u p", u=2)
                     for u in range(2):
-                        nc.tensor.transpose(
-                            bank[:, u, r * P : (r + 1) * P], words[:, u * P : (u + 1) * P], identity[:]
-                        )
+                        nc.tensor.transpose(bank[:, u, r * P : (r + 1) * P], words[:, u, :], identity[:])
                 banks.append(bank)
             return banks
 
@@ -143,12 +135,13 @@ def tile_cnl_pb_kernel(
             return g_grouped
 
         def add_shift(b, channel_tiles, on_vector):
+            vector_tiles = TILES_ON_VECTOR if b + 2 < IMAGES else 0
             for ct in channel_tiles:
-                if on_vector and ct < TILES_ON_VECTOR:
+                if on_vector and ct < vector_tiles:
                     nc.vector.tensor_scalar_add(
                         results[b][:, ct, :], x_tiles[b][:, ct, :], shift[:, ct : ct + 1]
                     )
-                if not on_vector and ct >= TILES_ON_VECTOR:
+                if not on_vector and ct >= vector_tiles:
                     nc.scalar.activation(
                         out=results[b][:, ct, :],
                         in_=x_tiles[b][:, ct, :],

@@ -21,6 +21,7 @@ ROW_TILES = CHANNELS // P
 EPS = 1e-5
 TILES_ON_VECTOR = 2
 EARLY_TILES = 2
+HEAD_PIECES = 2
 
 FLOPS = 2 * IMAGES * (CHANNELS * K * POSITIONS + CHANNELS * K * POSITIONS)
 
@@ -59,20 +60,35 @@ def tile_cnl_pb_kernel(
         nc.scalar.sqrt(warm[:], warm[:])
 
         att_tiles, g_tiles, x_tiles = [], [], []
+        att_loads, g_loads = [], []
         for b in range(IMAGES):
-            att_rows = resident.tile([P, PACK, K], BF16)
-            g_rows = resident.tile([P, PACK, POSITIONS], BF16)
+            pieces = HEAD_PIECES if b == 0 else 1
+            rows_a_piece = PACK // pieces
+            columns_a_piece = POSITIONS // pieces
+            att_tiles.append([])
+            g_tiles.append([])
+            att_loads.append([])
+            g_loads.append([])
+            for h in range(pieces):
+                att_rows = resident.tile([P, rows_a_piece, K], BF16, name="att_rows_%d" % pieces)
+                g_rows = resident.tile([P, PACK, columns_a_piece], BF16, name="g_rows_%d" % pieces)
+                att_tiles[b].extend([att_rows[:, r, :] for r in range(rows_a_piece)])
+                g_tiles[b].append((h * columns_a_piece, columns_a_piece, g_rows))
+                att_loads[b].append(
+                    (att_rows, k_on_partitions(attention[b])[:, h * rows_a_piece : (h + 1) * rows_a_piece, :])
+                )
+                g_loads[b].append(
+                    (g_rows, k_on_partitions(g_x[b])[:, :, h * columns_a_piece : (h + 1) * columns_a_piece])
+                )
             x_rows = resident.tile([P, ROW_TILES, POSITIONS], BF16)
-            att_tiles.append(att_rows)
-            g_tiles.append(g_rows)
             x_tiles.append(x_rows)
         w_rows = const.tile([P, ROW_TILES, K], BF16)
 
-        def load_attention(b):
-            nc.sync.dma_start(out=att_tiles[b][:], in_=k_on_partitions(attention[b]))
+        def load_attention(b, h=0):
+            nc.sync.dma_start(out=att_loads[b][h][0][:], in_=att_loads[b][h][1])
 
-        def load_g(b):
-            nc.sync.dma_start(out=g_tiles[b][:], in_=k_on_partitions(g_x[b]))
+        def load_g(b, h=0):
+            nc.sync.dma_start(out=g_loads[b][h][0][:], in_=g_loads[b][h][1])
 
         def load_x(b):
             nc.sync.dma_start(
@@ -80,8 +96,9 @@ def tile_cnl_pb_kernel(
                 in_=x[b].rearrange("(p ct) h w -> p ct (h w)", ct=ROW_TILES),
             )
 
-        load_attention(0)
-        load_g(0)
+        for h in range(HEAD_PIECES):
+            load_attention(0, h)
+            load_g(0, h)
         nc.sync.dma_start(out=w_rows[:], in_=Ww.rearrange("(p ct) k -> p ct k", ct=ROW_TILES))
         load_attention(1)
         load_g(1)
@@ -106,7 +123,7 @@ def tile_cnl_pb_kernel(
             for first in range(0, ROW_TILES, 2):
                 bank = psum_front.tile([P, 2, 2 * P], F32, tag="front")
                 for r in range(2):
-                    words = rows[:, first + r, :].bitcast(F32).rearrange("m (p u) -> m u p", u=2)
+                    words = rows[first + r].bitcast(F32).rearrange("m (p u) -> m u p", u=2)
                     for u in range(2):
                         nc.tensor.transpose(bank[:, u, r * P : (r + 1) * P], words[:, u, :], identity[:])
                 banks.append(bank)
@@ -128,10 +145,13 @@ def tile_cnl_pb_kernel(
 
         def regroup_g(b):
             g_grouped = work.tile([P, POSITIONS, PACK], BF16, align_bytes=64)
-            nc.vector.tensor_copy(
-                out=g_grouped[:].rearrange("p (c i) t -> p c t i", i=4),
-                in_=g_tiles[b][:].rearrange("p t (c i) -> p c t i", i=4),
-            )
+            for first, width, g_rows in g_tiles[b]:
+                nc.vector.tensor_copy(
+                    out=g_grouped[:, first : first + width, :].rearrange(
+                        "p (c i) t -> p c t i", i=4
+                    ),
+                    in_=g_rows[:].rearrange("p t (c i) -> p c t i", i=4),
+                )
             return g_grouped
 
         def add_shift(b, channel_tiles, on_vector):
@@ -219,10 +239,6 @@ def tile_cnl_pb_kernel(
         results = {}
         for b in range(IMAGES):
             results[b] = resident.tile([P, ROW_TILES, POSITIONS], F32, name="result")
-        att_grouped = group_attention(transpose_words(att_tiles[0]))
-        g_grouped = regroup_g(0)
-        g_q = quantise_g(g_grouped)
-        operands[0] = (quantise(att_grouped[:], "att"), g_q)
         nc.vector.tensor_scalar_add(gain[:], per_channel["run_var"][:], EPS)
         nc.scalar.sqrt(gain[:], gain[:])
         nc.vector.tensor_sub(shift[:], per_channel["bw"][:], per_channel["run_mean"][:])
@@ -230,7 +246,11 @@ def tile_cnl_pb_kernel(
         nc.vector.tensor_mul(gain[:], gain[:], per_channel["gamma"][:])
         nc.vector.tensor_mul(shift[:], shift[:], gain[:])
         nc.vector.tensor_add(shift[:], shift[:], per_channel["beta"][:])
-        w_banks = transpose_words(w_rows)
+        att_grouped = group_attention(transpose_words(att_tiles[0]))
+        g_grouped = regroup_g(0)
+        att_q = quantise(att_grouped[:], "att")
+        operands[0] = (att_q, quantise_g(g_grouped))
+        w_banks = transpose_words([w_rows[:, ct, :] for ct in range(ROW_TILES)])
         interleave_halves(w_banks, w_grouped[:])
         g_grouped = regroup_g(1)
         nc.vector.quantize_mx(out=w_codes[:].bitcast(FP8X4), scales=w_scales[:], in_=w_grouped[:])

@@ -57,7 +57,7 @@ def tile_cnl_pb_kernel(
 
         warm = const.tile([P, 1], F32)
         nc.vector.memset(warm[:], 1.0)
-        nc.scalar.sqrt(warm[:], warm[:])
+        nc.scalar.activation(out=warm[:], in_=warm[:], func=ACT.Identity, bias=0.0, scale=1.0)
 
         att_tiles, g_tiles, x_tiles = [], [], []
         att_loads, g_loads = [], []
@@ -114,6 +114,7 @@ def tile_cnl_pb_kernel(
 
         gain = const.tile([P, ROW_TILES], F32)
         shift = const.tile([P, ROW_TILES], F32)
+        minus_half = const.tile([P, ROW_TILES], F32)
         w_grouped = const.tile([P, CHANNELS * PACK], BF16, align_bytes=64)
         w_codes = const.tile([P, CHANNELS], U32, align_bytes=64)
         w_scales = const.tile([P, CHANNELS], U8, align_bytes=64)
@@ -239,13 +240,17 @@ def tile_cnl_pb_kernel(
         results = {}
         for b in range(IMAGES):
             results[b] = resident.tile([P, ROW_TILES, POSITIONS], F32, name="result")
-        nc.vector.tensor_scalar_add(gain[:], per_channel["run_var"][:], EPS)
-        nc.scalar.sqrt(gain[:], gain[:])
-        nc.vector.tensor_sub(shift[:], per_channel["bw"][:], per_channel["run_mean"][:])
-        nc.vector.reciprocal(gain[:], gain[:])
-        nc.vector.tensor_mul(gain[:], gain[:], per_channel["gamma"][:])
-        nc.vector.tensor_mul(shift[:], shift[:], gain[:])
-        nc.vector.tensor_add(shift[:], shift[:], per_channel["beta"][:])
+        nc.gpsimd.memset(minus_half[:], -0.5)
+        nc.gpsimd.tensor_scalar(
+            out=gain[:], in0=per_channel["run_var"][:], scalar1=1.0, scalar2=EPS, op0=ALU.mult, op1=ALU.add
+        )
+        nc.gpsimd.tensor_tensor(out=gain[:], in0=gain[:], in1=minus_half[:], op=ALU.pow)
+        nc.gpsimd.tensor_tensor(out=gain[:], in0=gain[:], in1=per_channel["gamma"][:], op=ALU.mult)
+        nc.gpsimd.tensor_tensor(
+            out=shift[:], in0=per_channel["bw"][:], in1=per_channel["run_mean"][:], op=ALU.subtract
+        )
+        nc.gpsimd.tensor_tensor(out=shift[:], in0=shift[:], in1=gain[:], op=ALU.mult)
+        nc.gpsimd.tensor_tensor(out=shift[:], in0=shift[:], in1=per_channel["beta"][:], op=ALU.add)
         att_grouped = group_attention(transpose_words(att_tiles[0]))
         g_grouped = regroup_g(0)
         att_q = quantise(att_grouped[:], "att")

@@ -21,6 +21,7 @@ ROW_TILES = CHANNELS // P
 EPS = 1e-5
 TILES_ON_VECTOR = 2
 EARLY_TILES = 2
+LAST_PIECES = 2
 HEAD_PIECES = 2
 
 FLOPS = 2 * IMAGES * (CHANNELS * K * POSITIONS + CHANNELS * K * POSITIONS)
@@ -145,7 +146,8 @@ def tile_cnl_pb_kernel(
             return codes, scales
 
         def regroup_g(b):
-            g_grouped = work.tile([P, POSITIONS, PACK], BF16, align_bytes=64)
+            pair_grouped = work.tile([P, 2 * K * PACK], BF16, align_bytes=64)
+            g_grouped = pair_grouped[:, K * PACK :].rearrange("p (n t) -> p n t", t=PACK)
             for first, width, g_rows in g_tiles[b]:
                 nc.vector.tensor_copy(
                     out=g_grouped[:, first : first + width, :].rearrange(
@@ -153,7 +155,13 @@ def tile_cnl_pb_kernel(
                     ),
                     in_=g_rows[:].rearrange("p t (c i) -> p c t i", i=4),
                 )
-            return g_grouped
+            return pair_grouped
+
+        def quantise_pair(pair_grouped):
+            codes = work.tile([P, 2 * CHANNELS], U32, align_bytes=64, name="pair_codes")
+            scales = work.tile([P, 2 * CHANNELS], U8, align_bytes=64, name="pair_scales")
+            nc.vector.quantize_mx(out=codes[:].bitcast(FP8X4), scales=scales[:], in_=pair_grouped[:])
+            return codes, scales
 
         def add_shift(b, channel_tiles, on_vector):
             vector_tiles = TILES_ON_VECTOR if b + 2 < IMAGES else 0
@@ -171,17 +179,17 @@ def tile_cnl_pb_kernel(
                         scale=1.0,
                     )
 
-        def first_product(att_q, g_q):
+        def first_product(pair_q):
             y_banks = []
             for n0 in range(0, POSITIONS, P):
                 y_bank = psum_front.tile([P, PACK, P], F32, tag="front")
                 for t in range(PACK):
                     nc.tensor.matmul_mx(
                         out=y_bank[:, t, :],
-                        lhsT=att_q[0][:, t * P : (t + 1) * P].bitcast(FP8X4),
-                        lhsT_scale=att_q[1][:, t * P : (t + 1) * P],
-                        rhs=g_q[0][:, n0 : n0 + P].bitcast(FP8X4),
-                        rhs_scale=g_q[1][:, n0 : n0 + P],
+                        lhsT=pair_q[0][:, t * P : (t + 1) * P].bitcast(FP8X4),
+                        lhsT_scale=pair_q[1][:, t * P : (t + 1) * P],
+                        rhs=pair_q[0][:, CHANNELS + n0 : CHANNELS + n0 + P].bitcast(FP8X4),
+                        rhs_scale=pair_q[1][:, CHANNELS + n0 : CHANNELS + n0 + P],
                         start=True,
                         stop=True,
                     )
@@ -214,26 +222,25 @@ def tile_cnl_pb_kernel(
         def finish(b, channel_tiles):
             out_b = out[b].rearrange("(p ct) h w -> p ct (h w)", ct=ROW_TILES)
             for ct in channel_tiles:
-                nc.vector.scalar_tensor_tensor(
-                    out=results[b][:, ct, :],
-                    in0=z_banks[(b, ct)][:],
-                    scalar=gain[:, ct : ct + 1],
-                    in1=results[b][:, ct, :],
-                    op0=ALU.mult,
-                    op1=ALU.add,
-                )
-                nc.sync.dma_start(out=out_b[:, ct, :], in_=results[b][:, ct, :])
+                pieces = LAST_PIECES if (b, ct) == (IMAGES - 1, ROW_TILES - 1) else 1
+                width = POSITIONS // pieces
+                for first in range(0, POSITIONS, width):
+                    columns = slice(first, first + width)
+                    nc.vector.scalar_tensor_tensor(
+                        out=results[b][:, ct, columns],
+                        in0=z_banks[(b, ct)][:, columns],
+                        scalar=gain[:, ct : ct + 1],
+                        in1=results[b][:, ct, columns],
+                        op0=ALU.mult,
+                        op1=ALU.add,
+                    )
+                    nc.sync.dma_start(out=out_b[:, ct, columns], in_=results[b][:, ct, columns])
 
         early = range(EARLY_TILES)
         late = range(EARLY_TILES, ROW_TILES)
 
-        def group_attention(att_banks):
-            att_grouped = work.tile([P, CHANNELS * PACK], BF16, align_bytes=64)
-            interleave_halves(att_banks, att_grouped[:])
-            return att_grouped
-
-        def quantise_g(g_grouped):
-            return quantise(g_grouped[:].rearrange("p n t -> p (n t)"), "g")
+        def group_attention(att_banks, pair_grouped):
+            interleave_halves(att_banks, pair_grouped[:, 0 : K * PACK])
 
         operands = {}
         z_banks = {}
@@ -251,35 +258,32 @@ def tile_cnl_pb_kernel(
         )
         nc.gpsimd.tensor_tensor(out=shift[:], in0=shift[:], in1=gain[:], op=ALU.mult)
         nc.gpsimd.tensor_tensor(out=shift[:], in0=shift[:], in1=per_channel["beta"][:], op=ALU.add)
-        att_grouped = group_attention(transpose_words(att_tiles[0]))
-        g_grouped = regroup_g(0)
-        att_q = quantise(att_grouped[:], "att")
-        operands[0] = (att_q, quantise_g(g_grouped))
+        pairs = {0: regroup_g(0)}
+        group_attention(transpose_words(att_tiles[0]), pairs[0])
+        operands[0] = quantise_pair(pairs[0])
         w_banks = transpose_words([w_rows[:, ct, :] for ct in range(ROW_TILES)])
         interleave_halves(w_banks, w_grouped[:])
-        g_grouped = regroup_g(1)
+        pairs[1] = regroup_g(1)
         nc.vector.quantize_mx(out=w_codes[:].bitcast(FP8X4), scales=w_scales[:], in_=w_grouped[:])
-        att_grouped = group_attention(transpose_words(att_tiles[1]))
-        g_q = quantise_g(g_grouped)
-        operands[1] = (quantise(att_grouped[:], "att"), g_q)
-        g_grouped = regroup_g(2)
-        y_banks = first_product(operands[0][0], operands[0][1])
+        group_attention(transpose_words(att_tiles[1]), pairs[1])
+        operands[1] = quantise_pair(pairs[1])
+        pairs[2] = regroup_g(2)
+        y_banks = first_product(operands[0])
 
         for b in range(IMAGES + 1):
             if b < IMAGES:
                 y_grouped = round_y(y_banks)
             if b + 2 < IMAGES:
-                att_grouped = group_attention(transpose_words(att_tiles[b + 2]))
+                group_attention(transpose_words(att_tiles[b + 2]), pairs[b + 2])
             if b + 1 < IMAGES:
-                y_banks = first_product(operands[b + 1][0], operands[b + 1][1])
+                y_banks = first_product(operands[b + 1])
             if b > 0:
                 add_shift(b - 1, late, False)
             if b < IMAGES:
                 add_shift(b, early, False)
                 y_q = quantise(y_grouped[:].rearrange("p n t -> p (n t)"), "y")
             if b + 2 < IMAGES:
-                g_q = quantise_g(g_grouped)
-                operands[b + 2] = (quantise(att_grouped[:], "att"), g_q)
+                operands[b + 2] = quantise_pair(pairs[b + 2])
             if b < IMAGES:
                 second_product(b, y_q, early)
             if b > 0:
@@ -288,7 +292,7 @@ def tile_cnl_pb_kernel(
             if b < IMAGES:
                 second_product(b, y_q, late)
             if b + 3 < IMAGES:
-                g_grouped = regroup_g(b + 3)
+                pairs[b + 3] = regroup_g(b + 3)
             if b < IMAGES:
                 add_shift(b, early, True)
                 finish(b, early)

@@ -22,7 +22,7 @@ EPS = 1e-5
 TILES_ON_VECTOR = 2
 EARLY_TILES = 2
 LAST_PIECES = 2
-HEAD_PIECES = 2
+HEAD_PIECES = 1
 
 FLOPS = 2 * IMAGES * (CHANNELS * K * POSITIONS + CHANNELS * K * POSITIONS)
 

@@ -146,7 +146,7 @@ def tile_cnl_pb_kernel(
             return codes, scales
 
         def regroup_g(b):
-            pair_grouped = work.tile([P, 2 * K * PACK], BF16, align_bytes=64)
+            pair_grouped = work.tile([P, 2 * K * PACK], BF16, align_bytes=64, tag="pair_grouped")
             g_grouped = pair_grouped[:, K * PACK :].rearrange("p (n t) -> p n t", t=PACK)
             for first, width, g_rows in g_tiles[b]:
                 nc.vector.tensor_copy(
@@ -163,21 +163,26 @@ def tile_cnl_pb_kernel(
             nc.vector.quantize_mx(out=codes[:].bitcast(FP8X4), scales=scales[:], in_=pair_grouped[:])
             return codes, scales
 
-        def add_shift(b, channel_tiles, on_vector):
-            vector_tiles = TILES_ON_VECTOR if b + 2 < IMAGES else 0
-            for ct in channel_tiles:
-                if on_vector and ct < vector_tiles:
-                    nc.vector.tensor_scalar_add(
-                        results[b][:, ct, :], x_tiles[b][:, ct, :], shift[:, ct : ct + 1]
-                    )
-                if not on_vector and ct >= vector_tiles:
-                    nc.scalar.activation(
-                        out=results[b][:, ct, :],
-                        in_=x_tiles[b][:, ct, :],
-                        func=ACT.Identity,
-                        bias=shift[:, ct : ct + 1],
-                        scale=1.0,
-                    )
+        def add_shift(b, ct, engine):
+            if engine == "V":
+                nc.vector.tensor_scalar_add(res[(b, ct)], x_tiles[b][:, ct, :], shift[:, ct : ct + 1])
+            elif engine == "S":
+                nc.scalar.activation(
+                    out=res[(b, ct)],
+                    in_=x_tiles[b][:, ct, :],
+                    func=ACT.Identity,
+                    bias=shift[:, ct : ct + 1],
+                    scale=1.0,
+                )
+            else:
+                nc.gpsimd.tensor_scalar(
+                    out=res[(b, ct)],
+                    in0=x_tiles[b][:, ct, :],
+                    scalar1=1.0,
+                    scalar2=shift[:, ct : ct + 1],
+                    op0=ALU.mult,
+                    op1=ALU.add,
+                )
 
         def first_product(pair_q):
             y_banks = []
@@ -227,26 +232,31 @@ def tile_cnl_pb_kernel(
                 for first in range(0, POSITIONS, width):
                     columns = slice(first, first + width)
                     nc.vector.scalar_tensor_tensor(
-                        out=results[b][:, ct, columns],
+                        out=res[(b, ct)][:, columns],
                         in0=z_banks[(b, ct)][:, columns],
                         scalar=gain[:, ct : ct + 1],
-                        in1=results[b][:, ct, columns],
+                        in1=res[(b, ct)][:, columns],
                         op0=ALU.mult,
                         op1=ALU.add,
                     )
-                    nc.sync.dma_start(out=out_b[:, ct, columns], in_=results[b][:, ct, columns])
-
-        early = range(EARLY_TILES)
-        late = range(EARLY_TILES, ROW_TILES)
+                    nc.sync.dma_start(out=out_b[:, ct, columns], in_=res[(b, ct)][:, columns])
 
         def group_attention(att_banks, pair_grouped):
             interleave_halves(att_banks, pair_grouped[:, 0 : K * PACK])
 
         operands = {}
         z_banks = {}
-        results = {}
+        res = {}
         for b in range(IMAGES):
-            results[b] = resident.tile([P, ROW_TILES, POSITIONS], F32, name="result")
+            result = resident.tile([P, ROW_TILES, POSITIONS], F32, name="result")
+            for ct in range(ROW_TILES):
+                res[(b, ct)] = result[:, ct, :]
+
+        def gpsimd_tiles(b, channel_tiles):
+            shared = work.tile([P, len(channel_tiles), POSITIONS], F32, align_bytes=64, tag="pair_grouped")
+            for j, ct in enumerate(channel_tiles):
+                res[(b, ct)] = shared[:, j, :]
+                add_shift(b, ct, "G")
         nc.gpsimd.memset(minus_half[:], -0.5)
         nc.gpsimd.tensor_scalar(
             out=gain[:], in0=per_channel["run_var"][:], scalar1=1.0, scalar2=EPS, op0=ALU.mult, op1=ALU.add
@@ -270,29 +280,41 @@ def tile_cnl_pb_kernel(
         pairs[2] = regroup_g(2)
         y_banks = first_product(operands[0])
 
-        for b in range(IMAGES + 1):
-            if b < IMAGES:
-                y_grouped = round_y(y_banks)
-            if b + 2 < IMAGES:
-                group_attention(transpose_words(att_tiles[b + 2]), pairs[b + 2])
-            if b + 1 < IMAGES:
-                y_banks = first_product(operands[b + 1])
-            if b > 0:
-                add_shift(b - 1, late, False)
-            if b < IMAGES:
-                add_shift(b, early, False)
-                y_q = quantise(y_grouped[:].rearrange("p n t -> p (n t)"), "y")
-            if b + 2 < IMAGES:
-                operands[b + 2] = quantise_pair(pairs[b + 2])
-            if b < IMAGES:
-                second_product(b, y_q, early)
-            if b > 0:
-                add_shift(b - 1, late, True)
-                finish(b - 1, late)
-            if b < IMAGES:
-                second_product(b, y_q, late)
-            if b + 3 < IMAGES:
-                pairs[b + 3] = regroup_g(b + 3)
-            if b < IMAGES:
-                add_shift(b, early, True)
-                finish(b, early)
+        every = range(ROW_TILES)
+        y_grouped = round_y(y_banks)
+        group_attention(transpose_words(att_tiles[2]), pairs[2])
+        y_banks = first_product(operands[1])
+        for ct in every:
+            add_shift(0, ct, "S")
+        y_q = quantise(y_grouped[:].rearrange("p n t -> p (n t)"), "y")
+        pairs[3] = regroup_g(3)
+        operands[2] = quantise_pair(pairs[2])
+        second_product(0, y_q, every)
+        gpsimd_tiles(1, [0, 1])
+        finish(0, every)
+        y_grouped = round_y(y_banks)
+        group_attention(transpose_words(att_tiles[3]), pairs[3])
+        y_banks = first_product(operands[2])
+        add_shift(1, 2, "S")
+        add_shift(1, 3, "S")
+        y_q = quantise(y_grouped[:].rearrange("p n t -> p (n t)"), "y")
+        operands[3] = quantise_pair(pairs[3])
+        second_product(1, y_q, every)
+        gpsimd_tiles(2, [0, 1])
+        finish(1, every)
+        y_grouped = round_y(y_banks)
+        y_banks = first_product(operands[3])
+        y_q = quantise(y_grouped[:].rearrange("p n t -> p (n t)"), "y")
+        second_product(2, y_q, [0, 1])
+        y_grouped = round_y(y_banks)
+        finish(2, [0, 1])
+        second_product(2, y_q, [2, 3])
+        add_shift(2, 2, "S")
+        add_shift(2, 3, "S")
+        for ct in every:
+            add_shift(3, ct, "S")
+        y_q = quantise(y_grouped[:].rearrange("p n t -> p (n t)"), "y")
+        second_product(3, y_q, [0, 1])
+        finish(2, [2, 3])
+        second_product(3, y_q, [2, 3])
+        finish(3, every)

@@ -103,12 +103,14 @@ def tile_cnl_pb_kernel(
         nc.sync.dma_start(out=w_rows[:], in_=Ww.rearrange("(p ct) k -> p ct k", ct=ROW_TILES))
         load_attention(1)
         load_g(1)
-        for b in range(2, IMAGES):
-            load_g(b)
-            load_attention(b)
-            load_x(b - 2)
-        load_x(IMAGES - 2)
-        load_x(IMAGES - 1)
+        load_g(2)
+        load_attention(2)
+        load_x(0)
+        load_g(3)
+        load_x(1)
+        load_attention(3)
+        load_x(2)
+        load_x(3)
 
         identity = const.tile([P, P], F32)
         make_identity(nc, identity[:])
@@ -301,14 +303,15 @@ def tile_cnl_pb_kernel(
         operands[3] = quantise_pair(pairs[3])
         second_product(1, y_q, every)
         gpsimd_tiles(2, [0, 1])
-        finish(1, every)
+        finish(1, [0, 1, 2])
         y_grouped = round_y(y_banks)
         y_banks = first_product(operands[3])
         y_q = quantise(y_grouped[:].rearrange("p n t -> p (n t)"), "y")
-        second_product(2, y_q, [0, 1])
+        second_product(2, y_q, [0, 1, 2])
+        finish(1, [3])
         y_grouped = round_y(y_banks)
         finish(2, [0, 1])
-        second_product(2, y_q, [2, 3])
+        second_product(2, y_q, [3])
         add_shift(2, 2, "S")
         add_shift(2, 3, "S")
         for ct in every:

@@ -286,15 +286,15 @@ def tile_cnl_pb_kernel(
         y_grouped = round_y(y_banks)
         group_attention(transpose_words(att_tiles[2]), pairs[2])
         y_banks = first_product(operands[1])
-        for ct in every:
-            add_shift(0, ct, "S")
         y_q = quantise(y_grouped[:].rearrange("p n t -> p (n t)"), "y")
         pairs[3] = regroup_g(3)
         operands[2] = quantise_pair(pairs[2])
         second_product(0, y_q, every)
+        y_grouped = round_y(y_banks)
+        for ct in every:
+            add_shift(0, ct, "S")
         gpsimd_tiles(1, [0, 1])
         finish(0, every)
-        y_grouped = round_y(y_banks)
         group_attention(transpose_words(att_tiles[3]), pairs[3])
         y_banks = first_product(operands[2])
         add_shift(1, 2, "S")

@@ -103,10 +103,10 @@ def tile_cnl_pb_kernel(
         nc.sync.dma_start(out=w_rows[:], in_=Ww.rearrange("(p ct) k -> p ct k", ct=ROW_TILES))
         load_attention(1)
         load_g(1)
-        load_g(2)
         load_attention(2)
-        load_x(0)
+        load_g(2)
         load_g(3)
+        load_x(0)
         load_x(1)
         load_attention(3)
         load_x(2)

@@ -204,7 +204,7 @@ def tile_cnl_pb_kernel(
             return y_banks
 
         def round_y(y_banks):
-            y_grouped = work.tile([P, POSITIONS, PACK], BF16, align_bytes=64)
+            y_grouped = work.tile([P, POSITIONS, PACK], BF16, align_bytes=64, tag="y_grouped")
             for q, y_bank in enumerate(y_banks):
                 nc.scalar.copy(
                     out=y_grouped[:, q * P : (q + 1) * P, :],
@@ -254,8 +254,8 @@ def tile_cnl_pb_kernel(
             for ct in range(ROW_TILES):
                 res[(b, ct)] = result[:, ct, :]
 
-        def gpsimd_tiles(b, channel_tiles):
-            shared = work.tile([P, len(channel_tiles), POSITIONS], F32, align_bytes=64, tag="pair_grouped")
+        def gpsimd_tiles(b, channel_tiles, place="pair_grouped"):
+            shared = work.tile([P, len(channel_tiles), POSITIONS], F32, align_bytes=64, tag=place)
             for j, ct in enumerate(channel_tiles):
                 res[(b, ct)] = shared[:, j, :]
                 add_shift(b, ct, "G")
@@ -297,22 +297,22 @@ def tile_cnl_pb_kernel(
         finish(0, every)
         group_attention(transpose_words(att_tiles[3]), pairs[3])
         y_banks = first_product(operands[2])
-        add_shift(1, 2, "S")
-        add_shift(1, 3, "S")
         y_q = quantise(y_grouped[:].rearrange("p n t -> p (n t)"), "y")
         operands[3] = quantise_pair(pairs[3])
         second_product(1, y_q, every)
-        gpsimd_tiles(2, [0, 1])
-        finish(1, [0, 1, 2])
+        gpsimd_tiles(2, [0])
+        finish(1, [0, 1])
         y_grouped = round_y(y_banks)
         y_banks = first_product(operands[3])
+        add_shift(1, 2, "S")
+        add_shift(1, 3, "S")
         y_q = quantise(y_grouped[:].rearrange("p n t -> p (n t)"), "y")
-        second_product(2, y_q, [0, 1, 2])
-        finish(1, [3])
+        second_product(2, y_q, [0, 1])
         y_grouped = round_y(y_banks)
+        gpsimd_tiles(2, [1, 2], "y_grouped")
+        finish(1, [2, 3])
+        second_product(2, y_q, [2, 3])
         finish(2, [0, 1])
-        second_product(2, y_q, [3])
-        add_shift(2, 2, "S")
         add_shift(2, 3, "S")
         for ct in every:
             add_shift(3, ct, "S")

@@ -58,7 +58,11 @@ def tile_cnl_pb_kernel(
 
         warm = const.tile([P, 1], F32)
         nc.vector.memset(warm[:], 1.0)
-        nc.scalar.activation(out=warm[:], in_=warm[:], func=ACT.Identity, bias=0.0, scale=1.0)
+        nc.scalar.activation(out=warm[:], in_=warm[:], func=ACT.Abs_reciprocal_sqrt, bias=0.0, scale=1.0)
+        inverse_deviation = const.tile([P, ROW_TILES], F32)
+        nc.scalar.activation(
+            out=inverse_deviation[:], in_=per_channel["run_var"][:], func=ACT.Abs_reciprocal_sqrt, bias=EPS, scale=1.0
+        )
 
         att_tiles, g_tiles, x_tiles = [], [], []
         att_loads, g_loads = [], []
@@ -117,7 +121,6 @@ def tile_cnl_pb_kernel(
 
         gain = const.tile([P, ROW_TILES], F32)
         shift = const.tile([P, ROW_TILES], F32)
-        minus_half = const.tile([P, ROW_TILES], F32)
         w_grouped = const.tile([P, CHANNELS * PACK], BF16, align_bytes=64)
         w_codes = const.tile([P, CHANNELS], U32, align_bytes=64)
         w_scales = const.tile([P, CHANNELS], U8, align_bytes=64)
@@ -259,12 +262,7 @@ def tile_cnl_pb_kernel(
             for j, ct in enumerate(channel_tiles):
                 res[(b, ct)] = shared[:, j, :]
                 add_shift(b, ct, "G")
-        nc.gpsimd.memset(minus_half[:], -0.5)
-        nc.gpsimd.tensor_scalar(
-            out=gain[:], in0=per_channel["run_var"][:], scalar1=1.0, scalar2=EPS, op0=ALU.mult, op1=ALU.add
-        )
-        nc.gpsimd.tensor_tensor(out=gain[:], in0=gain[:], in1=minus_half[:], op=ALU.pow)
-        nc.gpsimd.tensor_tensor(out=gain[:], in0=gain[:], in1=per_channel["gamma"][:], op=ALU.mult)
+        nc.gpsimd.tensor_tensor(out=gain[:], in0=inverse_deviation[:], in1=per_channel["gamma"][:], op=ALU.mult)
         nc.gpsimd.tensor_tensor(
             out=shift[:], in0=per_channel["bw"][:], in1=per_channel["run_mean"][:], op=ALU.subtract
         )

@@ -44,17 +44,16 @@ def tile_cnl_pb_kernel(
         ctx.enter_context(tc.manual_schedule())
 
         per_channel = {}
-        for name, vector in (
-            ("run_var", run_var),
-            ("gamma", gamma),
-            ("bw", bw),
-            ("run_mean", run_mean),
-            ("beta", beta),
-        ):
+        vectors = {"run_var": run_var, "gamma": gamma, "bw": bw, "run_mean": run_mean, "beta": beta}
+        for name in ("run_var", "gamma", "bw", "run_mean", "beta"):
             per_channel[name] = const.tile([P, ROW_TILES], BF16, name=name)
-            nc.scalar.dma_start(
-                out=per_channel[name][:], in_=vector.rearrange("(p ct) -> p ct", ct=ROW_TILES)
+
+        def load_vector(queue, name):
+            queue.dma_start(
+                out=per_channel[name][:], in_=vectors[name].rearrange("(p ct) -> p ct", ct=ROW_TILES)
             )
+
+        load_vector(nc.scalar, "run_var")
 
         warm = const.tile([P, 1], F32)
         nc.vector.memset(warm[:], 1.0)
@@ -101,9 +100,10 @@ def tile_cnl_pb_kernel(
                 in_=x[b].rearrange("(p ct) h w -> p ct (h w)", ct=ROW_TILES),
             )
 
-        for h in range(HEAD_PIECES):
-            load_attention(0, h)
-            load_g(0, h)
+        load_attention(0)
+        for name in ("gamma", "bw", "run_mean", "beta"):
+            load_vector(nc.sync, name)
+        load_g(0)
         nc.sync.dma_start(out=w_rows[:], in_=Ww.rearrange("(p ct) k -> p ct k", ct=ROW_TILES))
         load_attention(1)
         load_g(1)

from contextlib import ExitStack

import concourse.mybir as mybir
from concourse.masks import make_identity

BF16 = mybir.dt.bfloat16
F32 = mybir.dt.float32
U32 = mybir.dt.uint32
U8 = mybir.dt.uint8
FP8X4 = mybir.dt.float8_e4m3fn_x4
ALU = mybir.AluOpType
ACT = mybir.ActivationFunctionType

P = 128
PACK = 4
K = P * PACK
IMAGES = 4
CHANNELS = 512
POSITIONS = 512
ROW_TILES = CHANNELS // P
EPS = 1e-5
TILES_ON_VECTOR = 2
EARLY_TILES = 2
LAST_PIECES = 2
HEAD_PIECES = 1

FLOPS = 2 * IMAGES * (CHANNELS * K * POSITIONS + CHANNELS * K * POSITIONS)


def k_on_partitions(rows_in_dram):
    return rows_in_dram.rearrange("(p t) w -> p t w", t=PACK)


def tile_cnl_pb_kernel(
    tc, attention, g_x, x, Ww, bw, gamma, beta, run_mean, run_var, out
):
    nc = tc.nc
    with ExitStack() as ctx:
        const = ctx.enter_context(tc.tile_pool(name="const", bufs=1))
        resident = ctx.enter_context(tc.tile_pool(name="resident", bufs=IMAGES))
        work = ctx.enter_context(tc.tile_pool(name="work", bufs=2))
        psum_front = ctx.enter_context(tc.psum_pool(name="psum_front", bufs=4))
        psum_z = ctx.enter_context(tc.psum_pool(name="psum_z", bufs=ROW_TILES))
        ctx.enter_context(tc.manual_schedule())

        per_channel = {}
        vectors = {"run_var": run_var, "gamma": gamma, "bw": bw, "run_mean": run_mean, "beta": beta}
        for name in ("run_var", "gamma", "bw", "run_mean", "beta"):
            per_channel[name] = const.tile([P, ROW_TILES], BF16, name=name)

        def load_vector(queue, name):
            queue.dma_start(
                out=per_channel[name][:], in_=vectors[name].rearrange("(p ct) -> p ct", ct=ROW_TILES)
            )

        load_vector(nc.scalar, "run_var")

        warm = const.tile([P, 1], F32)
        nc.vector.memset(warm[:], 1.0)
        nc.scalar.activation(out=warm[:], in_=warm[:], func=ACT.Abs_reciprocal_sqrt, bias=0.0, scale=1.0)
        inverse_deviation = const.tile([P, ROW_TILES], F32)
        nc.scalar.activation(
            out=inverse_deviation[:], in_=per_channel["run_var"][:], func=ACT.Abs_reciprocal_sqrt, bias=EPS, scale=1.0
        )

        att_tiles, g_tiles, x_tiles = [], [], []
        att_loads, g_loads = [], []
        for b in range(IMAGES):
            pieces = HEAD_PIECES if b == 0 else 1
            rows_a_piece = PACK // pieces
            columns_a_piece = POSITIONS // pieces
            att_tiles.append([])
            g_tiles.append([])
            att_loads.append([])
            g_loads.append([])
            for h in range(pieces):
                att_rows = resident.tile([P, rows_a_piece, K], BF16, name="att_rows_%d" % pieces)
                g_rows = resident.tile([P, PACK, columns_a_piece], BF16, name="g_rows_%d" % pieces)
                att_tiles[b].extend([att_rows[:, r, :] for r in range(rows_a_piece)])
                g_tiles[b].append((h * columns_a_piece, columns_a_piece, g_rows))
                att_loads[b].append(
                    (att_rows, k_on_partitions(attention[b])[:, h * rows_a_piece : (h + 1) * rows_a_piece, :])
                )
                g_loads[b].append(
                    (g_rows, k_on_partitions(g_x[b])[:, :, h * columns_a_piece : (h + 1) * columns_a_piece])
                )
            x_rows = resident.tile([P, ROW_TILES, POSITIONS], BF16)
            x_tiles.append(x_rows)
        w_rows = const.tile([P, ROW_TILES, K], BF16)

        def load_attention(b, h=0):
            nc.sync.dma_start(out=att_loads[b][h][0][:], in_=att_loads[b][h][1])

        def load_g(b, h=0):
            nc.sync.dma_start(out=g_loads[b][h][0][:], in_=g_loads[b][h][1])

        def load_x(b):
            nc.sync.dma_start(
                out=x_tiles[b][:],
                in_=x[b].rearrange("(p ct) h w -> p ct (h w)", ct=ROW_TILES),
            )

        load_attention(0)
        for name in ("gamma", "bw", "run_mean", "beta"):
            load_vector(nc.sync, name)
        load_g(0)
        nc.sync.dma_start(out=w_rows[:], in_=Ww.rearrange("(p ct) k -> p ct k", ct=ROW_TILES))
        load_attention(1)
        load_g(1)
        load_attention(2)
        load_g(2)
        load_g(3)
        load_x(0)
        load_x(1)
        load_attention(3)
        load_x(2)
        load_x(3)

        identity = const.tile([P, P], F32)
        make_identity(nc, identity[:])

        gain = const.tile([P, ROW_TILES], F32)
        shift = const.tile([P, ROW_TILES], F32)
        w_grouped = const.tile([P, CHANNELS * PACK], BF16, align_bytes=64)
        w_codes = const.tile([P, CHANNELS], U32, align_bytes=64)
        w_scales = const.tile([P, CHANNELS], U8, align_bytes=64)

        def transpose_words(rows):
            banks = []
            for first in range(0, ROW_TILES, 2):
                bank = psum_front.tile([P, 2, 2 * P], F32, tag="front")
                for r in range(2):
                    words = rows[first + r].bitcast(F32).rearrange("m (p u) -> m u p", u=2)
                    for u in range(2):
                        nc.tensor.transpose(bank[:, u, r * P : (r + 1) * P], words[:, u, :], identity[:])
                banks.append(bank)
            return banks

        def interleave_halves(banks, grouped):
            grouped_words = grouped.bitcast(F32).rearrange("p (c u) -> p c u", u=2)
            for h, bank in enumerate(banks):
                nc.scalar.copy(
                    out=grouped_words[:, h * 2 * P : (h + 1) * 2 * P, :],
                    in_=bank[:].rearrange("p u c -> p c u"),
                )

        def quantise(grouped, operand):
            codes = work.tile([P, CHANNELS], U32, align_bytes=64, name=operand + "_codes")
            scales = work.tile([P, CHANNELS], U8, align_bytes=64, name=operand + "_scales")
            nc.vector.quantize_mx(out=codes[:].bitcast(FP8X4), scales=scales[:], in_=grouped)
            return codes, scales

        def regroup_g(b):
            pair_grouped = work.tile([P, 2 * K * PACK], BF16, align_bytes=64, tag="pair_grouped")
            g_grouped = pair_grouped[:, K * PACK :].rearrange("p (n t) -> p n t", t=PACK)
            for first, width, g_rows in g_tiles[b]:
                nc.vector.tensor_copy(
                    out=g_grouped[:, first : first + width, :].rearrange(
                        "p (c i) t -> p c t i", i=4
                    ),
                    in_=g_rows[:].rearrange("p t (c i) -> p c t i", i=4),
                )
            return pair_grouped

        def quantise_pair(pair_grouped):
            codes = work.tile([P, 2 * CHANNELS], U32, align_bytes=64, name="pair_codes")
            scales = work.tile([P, 2 * CHANNELS], U8, align_bytes=64, name="pair_scales")
            nc.vector.quantize_mx(out=codes[:].bitcast(FP8X4), scales=scales[:], in_=pair_grouped[:])
            return codes, scales

        def add_shift(b, ct, engine):
            if engine == "V":
                nc.vector.tensor_scalar_add(res[(b, ct)], x_tiles[b][:, ct, :], shift[:, ct : ct + 1])
            elif engine == "S":
                nc.scalar.activation(
                    out=res[(b, ct)],
                    in_=x_tiles[b][:, ct, :],
                    func=ACT.Identity,
                    bias=shift[:, ct : ct + 1],
                    scale=1.0,
                )
            else:
                nc.gpsimd.tensor_scalar(
                    out=res[(b, ct)],
                    in0=x_tiles[b][:, ct, :],
                    scalar1=1.0,
                    scalar2=shift[:, ct : ct + 1],
                    op0=ALU.mult,
                    op1=ALU.add,
                )

        def first_product(pair_q):
            y_banks = []
            for n0 in range(0, POSITIONS, P):
                y_bank = psum_front.tile([P, PACK, P], F32, tag="front")
                for t in range(PACK):
                    nc.tensor.matmul_mx(
                        out=y_bank[:, t, :],
                        lhsT=pair_q[0][:, t * P : (t + 1) * P].bitcast(FP8X4),
                        lhsT_scale=pair_q[1][:, t * P : (t + 1) * P],
                        rhs=pair_q[0][:, CHANNELS + n0 : CHANNELS + n0 + P].bitcast(FP8X4),
                        rhs_scale=pair_q[1][:, CHANNELS + n0 : CHANNELS + n0 + P],
                        start=True,
                        stop=True,
                    )
                y_banks.append(y_bank)
            return y_banks

        def round_y(y_banks):
            y_grouped = work.tile([P, POSITIONS, PACK], BF16, align_bytes=64, tag="y_grouped")
            for q, y_bank in enumerate(y_banks):
                nc.scalar.copy(
                    out=y_grouped[:, q * P : (q + 1) * P, :],
                    in_=y_bank[:].rearrange("p t n -> p n t"),
                )
            return y_grouped

        def second_product(b, y_q, channel_tiles):
            for ct in channel_tiles:
                z_bank = psum_z.tile([P, POSITIONS], F32)
                nc.tensor.matmul_mx(
                    out=z_bank[:],
                    lhsT=w_codes[:, ct * P : (ct + 1) * P].bitcast(FP8X4),
                    lhsT_scale=w_scales[:, ct * P : (ct + 1) * P],
                    rhs=y_q[0][:].bitcast(FP8X4),
                    rhs_scale=y_q[1][:],
                    start=True,
                    stop=True,
                )
                z_banks[(b, ct)] = z_bank

        def finish(b, channel_tiles):
            out_b = out[b].rearrange("(p ct) h w -> p ct (h w)", ct=ROW_TILES)
            for ct in channel_tiles:
                pieces = LAST_PIECES if (b, ct) == (IMAGES - 1, ROW_TILES - 1) else 1
                width = POSITIONS // pieces
                for first in range(0, POSITIONS, width):
                    columns = slice(first, first + width)
                    nc.vector.scalar_tensor_tensor(
                        out=res[(b, ct)][:, columns],
                        in0=z_banks[(b, ct)][:, columns],
                        scalar=gain[:, ct : ct + 1],
                        in1=res[(b, ct)][:, columns],
                        op0=ALU.mult,
                        op1=ALU.add,
                    )
                    nc.sync.dma_start(out=out_b[:, ct, columns], in_=res[(b, ct)][:, columns])

        def group_attention(att_banks, pair_grouped):
            interleave_halves(att_banks, pair_grouped[:, 0 : K * PACK])

        operands = {}
        z_banks = {}
        res = {}
        for b in range(IMAGES):
            result = resident.tile([P, ROW_TILES, POSITIONS], F32, name="result")
            for ct in range(ROW_TILES):
                res[(b, ct)] = result[:, ct, :]

        def gpsimd_tiles(b, channel_tiles, place="pair_grouped"):
            shared = work.tile([P, len(channel_tiles), POSITIONS], F32, align_bytes=64, tag=place)
            for j, ct in enumerate(channel_tiles):
                res[(b, ct)] = shared[:, j, :]
                add_shift(b, ct, "G")
        nc.gpsimd.tensor_tensor(out=gain[:], in0=inverse_deviation[:], in1=per_channel["gamma"][:], op=ALU.mult)
        nc.gpsimd.tensor_tensor(
            out=shift[:], in0=per_channel["bw"][:], in1=per_channel["run_mean"][:], op=ALU.subtract
        )
        nc.gpsimd.tensor_tensor(out=shift[:], in0=shift[:], in1=gain[:], op=ALU.mult)
        nc.gpsimd.tensor_tensor(out=shift[:], in0=shift[:], in1=per_channel["beta"][:], op=ALU.add)
        pairs = {0: regroup_g(0)}
        group_attention(transpose_words(att_tiles[0]), pairs[0])
        operands[0] = quantise_pair(pairs[0])
        w_banks = transpose_words([w_rows[:, ct, :] for ct in range(ROW_TILES)])
        interleave_halves(w_banks, w_grouped[:])
        pairs[1] = regroup_g(1)
        nc.vector.quantize_mx(out=w_codes[:].bitcast(FP8X4), scales=w_scales[:], in_=w_grouped[:])
        group_attention(transpose_words(att_tiles[1]), pairs[1])
        operands[1] = quantise_pair(pairs[1])
        pairs[2] = regroup_g(2)
        y_banks = first_product(operands[0])

        every = range(ROW_TILES)
        y_grouped = round_y(y_banks)
        group_attention(transpose_words(att_tiles[2]), pairs[2])
        y_banks = first_product(operands[1])
        y_q = quantise(y_grouped[:].rearrange("p n t -> p (n t)"), "y")
        pairs[3] = regroup_g(3)
        operands[2] = quantise_pair(pairs[2])
        second_product(0, y_q, every)
        y_grouped = round_y(y_banks)
        for ct in every:
            add_shift(0, ct, "S")
        gpsimd_tiles(1, [0, 1])
        finish(0, every)
        group_attention(transpose_words(att_tiles[3]), pairs[3])
        y_banks = first_product(operands[2])
        y_q = quantise(y_grouped[:].rearrange("p n t -> p (n t)"), "y")
        operands[3] = quantise_pair(pairs[3])
        second_product(1, y_q, every)
        gpsimd_tiles(2, [0])
        finish(1, [0, 1])
        y_grouped = round_y(y_banks)
        y_banks = first_product(operands[3])
        add_shift(1, 2, "S")
        add_shift(1, 3, "S")
        y_q = quantise(y_grouped[:].rearrange("p n t -> p (n t)"), "y")
        second_product(2, y_q, [0, 1])
        y_grouped = round_y(y_banks)
        gpsimd_tiles(2, [1, 2], "y_grouped")
        finish(1, [2, 3])
        second_product(2, y_q, [2, 3])
        finish(2, [0, 1])
        add_shift(2, 3, "S")
        for ct in every:
            add_shift(3, ct, "S")
        y_q = quantise(y_grouped[:].rearrange("p n t -> p (n t)"), "y")
        second_product(3, y_q, [0, 1])
        finish(2, [2, 3])
        second_product(3, y_q, [2, 3])
        finish(3, every)
